import numpy as np
import ml_dtypes


def mxq(x, axis, fmt="e4m3"):
    dtype, down = {"e4m3": (ml_dtypes.float8_e4m3fn, 7), "e5m2": (ml_dtypes.float8_e5m2, 14)}[fmt]
    v = np.moveaxis(np.asarray(x, np.float32).astype(ml_dtypes.bfloat16).astype(np.float64), axis, -1)
    blocks = v.reshape(v.shape[:-1] + (-1, 32))
    amax = np.abs(blocks).max(-1, keepdims=True)
    byte = np.maximum(np.where(amax > 0, np.frexp(amax)[1] - 1 + 127, 0) - down, 1)
    scale = np.exp2(byte - 127.0)
    codes = (blocks / scale).astype(np.float32).astype(dtype).astype(np.float64)
    return np.moveaxis((codes * scale).reshape(v.shape), -1, axis)


WIDE = False


def mx_kscale(k):
    if not WIDE:
        return np.ones(k)
    levels = np.array([18, -18])
    if k % 512:
        return np.exp2(np.random.permutation(np.resize(levels, k // 32))).repeat(32)
    a = np.empty((k // 512, 16))
    for p in range(k // 512):
        a[p, :8] = np.random.permutation(np.resize(levels, 8))
        for g in range(8):
            far = levels[np.abs(levels - a[p, g]) >= 10]
            a[p, g + 8] = far[np.random.randint(len(far))]
    return np.exp2(a.ravel()).repeat(32)


BF16 = ml_dtypes.bfloat16


def bf(x):
    return np.asarray(x, np.float32).astype(BF16)


def f64(x):
    return np.asarray(x).astype(np.float64)


B, U = 1024, 1024
MASK_DENSITY = 1.0 / 16.0
W_STD = 1.0 / np.sqrt(U * MASK_DENSITY)


def setup_inputs():
    s = mx_kscale(B)[:, None]
    u = mx_kscale(U)
    v = mx_kscale(U)
    h0_0 = bf(np.random.standard_normal((B, U)))
    k1_0 = bf(np.random.standard_normal((U, U)) * W_STD)
    k2_0 = bf(np.random.standard_normal((U, U)) * W_STD)
    m1 = bf(np.random.random((U, U)) < MASK_DENSITY)
    m2 = bf(np.random.random((U, U)) < MASK_DENSITY)
    scaling = bf(np.random.uniform(1.25, 1.75, 1))
    bias = bf(np.random.standard_normal(U) * 0.5)
    g = bf(np.random.standard_normal((B, U)) * np.exp2(np.random.randint(-6, 1, (B, 1))) / s * u)
    h1 = f64(h0_0) @ (f64(k1_0) * f64(m1))
    z = f64(scaling) * (h1 @ (f64(k2_0) * f64(m2))) + f64(bias)
    return {"h0": bf(f64(h0_0) * s),
            "k1": bf(f64(k1_0) / v),
            "k2": bf(f64(k2_0) * v[:, None] / u),
            "m1": m1,
            "m2": m2,
            "scaling": scaling,
            "bias": bias,
            "z": np.asarray(z, np.float32),
            "grad_out": g}


def reference(h0, k1, k2, m1, m2, scaling, bias, z, grad_out):
    m1f = f64(m1)
    w1 = f64(k1) * m1f
    w2 = f64(k2) * f64(m2)
    dz2 = f64(grad_out) * (f64(z) > 0.0) * f64(scaling)
    dz1 = mxq(dz2, 1, "e5m2") @ mxq(w2, 1, "e4m3").T
    dh0 = mxq(dz1, 1, "e5m2") @ mxq(w1, 1, "e4m3").T
    dw1 = mxq(f64(h0), 0, "e4m3").T @ mxq(dz1, 0, "e5m2")
    return dh0, dw1 * m1f

@@ -1,0 +1,387 @@
+from contextlib import ExitStack
+
+import concourse.mybir as mybir
+from concourse.masks import make_identity
+
+FLOPS = 3 * 2 * 1024 * 1024 * 1024
+
+F32 = mybir.dt.float32
+BF16 = mybir.dt.bfloat16
+U32 = mybir.dt.uint32
+U8 = mybir.dt.uint8
+E4 = mybir.dt.float8_e4m3fn_x4
+E5 = mybir.dt.float8_e5m2_x4
+ALU = mybir.AluOpType
+
+P = 128
+U = 1024
+HALF = 512
+
+
+def tile_sparsefactorisationdense_pa_v_kernel(
+    tc, h0, k1, k2, m1, m2, scaling, bias, z, grad_out, out_0, out_1
+):
+    nc = tc.nc
+    k1_v = k1.rearrange("(c a p) w -> c p a w", a=2, p=P)
+    k2_v = k2.rearrange("(c a p) w -> c p a w", a=2, p=P)
+    m1_v = m1.rearrange("(c a p) w -> c p a w", a=2, p=P)
+    m2_v = m2.rearrange("(c a p) w -> c p a w", a=2, p=P)
+    z_v = z.rearrange("(b p s) w -> b p s w", p=P, s=4)
+    g_v = grad_out.rearrange("(b p s) w -> b p s w", p=P, s=4)
+    h_v = h0.rearrange("(b p s) w -> b p s w", p=P, s=4)
+    out_0_v = out_0.rearrange("(b p s) w -> b p s w", p=P, s=4)
+    out_1_v = out_1.rearrange("(t p) w -> t p w", p=P)
+
+    with ExitStack() as ctx:
+        const = ctx.enter_context(tc.tile_pool(name="const", bufs=1))
+        raw8 = ctx.enter_context(tc.tile_pool(name="raw8", bufs=3))
+        raw_h = ctx.enter_context(tc.tile_pool(name="raw_h", bufs=4))
+        raw4 = ctx.enter_context(tc.tile_pool(name="raw4", bufs=3))
+        keep_m = ctx.enter_context(tc.tile_pool(name="keep_m", bufs=4))
+        mid = ctx.enter_context(tc.tile_pool(name="mid", bufs=2))
+        grps = ctx.enter_context(tc.tile_pool(name="grps", bufs=6))
+        keep = ctx.enter_context(tc.tile_pool(name="keep", bufs=1))
+        outs = ctx.enter_context(tc.tile_pool(name="outs", bufs=6))
+        ps_t = ctx.enter_context(tc.psum_pool(name="ps_t", bufs=3))
+        ps_m = ctx.enter_context(tc.psum_pool(name="ps_m", bufs=5))
+
+        ident = const.tile([P, P], F32, name="ident")
+        make_identity(nc, ident[:])
+        ident_b = const.tile([P, P], BF16, name="ident_b")
+        make_identity(nc, ident_b[:])
+        gain_raw = const.tile([P, 1], BF16, name="gain_raw")
+        gain = const.tile([P, 1], F32, name="gain")
+
+        def codes(name, dims):
+            return (
+                keep.tile([P] + dims, U32, align_bytes=64, name=name + "_q"),
+                keep.tile([P] + dims, U8, align_bytes=64, name=name + "_s"),
+            )
+
+        w2_q, w2_s = codes("w2", [2, 2, HALF])
+        w1_q, w1_s = codes("w1", [2, 2, HALF])
+        z2_q, z2_s = codes("z2", [4, 2, 2, P])
+        dt_q, dt_s = codes("dt", [4, 2, 2, P])
+        db_q, db_s = codes("db", [2, 2, HALF])
+        h_q, h_s = codes("h", [2, 2, HALF])
+        dz1 = [keep.tile([P, 4, U], BF16, align_bytes=64, name="dz1_%d" % b) for b in range(2)]
+
+        def new_grp():
+            return grps.tile([P, 2048], BF16, align_bytes=64, name="grp")
+
+        def load(pool, name, shape, dtype, src):
+            t = pool.tile([P] + shape, dtype, name=name)
+            nc.sync.dma_start(out=t[:], in_=src)
+            return t
+
+        def sort_mult(dst, a, b):
+            nc.vector.tensor_tensor(
+                out=dst.rearrange("p u a (q r) -> p u (a q) r", r=16),
+                in0=a.rearrange("p a (q u r) -> p u (a q) r", u=2, r=16),
+                in1=b.rearrange("p a (q u r) -> p u (a q) r", u=2, r=16),
+                op=ALU.mult,
+            )
+
+        def leave(out, in_, on):
+            if on == "DVE":
+                nc.vector.tensor_copy(out=out, in_=in_)
+            else:
+                nc.scalar.copy(out=out, in_=in_)
+
+        def turn2(tr, k, half):
+            for u in range(2):
+                nc.tensor.transpose(tr[:, k + u, :], half(u).bitcast(F32), ident[:])
+
+        def mx(acc, lq, ls, rq, rs, ldt, rdt):
+            for g in range(2):
+                nc.tensor.matmul_mx(
+                    out=acc[:],
+                    lhsT=lq[g].bitcast(ldt),
+                    lhsT_scale=ls[g],
+                    rhs=rq[g].bitcast(rdt),
+                    rhs_scale=rs[g],
+                    start=(g == 0),
+                    stop=(g == 1),
+                )
+
+        prod, grp = {}, {}
+        k_sb, m_sb, z_sb, g_sb, h_sb = {}, {}, {}, {}, {}
+        codes_of = {1: (w1_q, w1_s), 2: (w2_q, w2_s)}
+
+        def wm(f, c):
+            w_sb = mid.tile([P, 2, 2, HALF], BF16, name="w_sb")
+            if (f, c, 0) in k_sb:
+                for a in range(2):
+                    sort_mult(w_sb[:, :, a : a + 1, :], k_sb[f, c, a][:], m_sb[f, c, a][:])
+            else:
+                sort_mult(w_sb[:], k_sb[f, c][:], m_sb[f, c][:])
+            prod["w", f, c] = w_sb
+
+        def wt(f, c, on="ACT"):
+            for g in range(2):
+                if (f, c // 2, g) not in grp:
+                    grp[f, c // 2, g] = new_grp()
+                tr = ps_t.tile([P, 4, P], F32, name="tr")
+                for a in range(2):
+                    turn2(tr, 2 * a, lambda u: prod["w", f, c][:, u, a, 256 * g : 256 * g + 256])
+                lo = 512 * (c % 2)
+                leave(
+                    grp[f, c // 2, g][:].bitcast(F32)[:, lo : lo + 512].rearrange("p (a r u) -> p a r u", a=2, u=2),
+                    tr[:].rearrange("p (a u) r -> p a r u", u=2),
+                    on,
+                )
+
+        def wq(f, half):
+            q, s = codes_of[f]
+            for g in range(2):
+                nc.vector.quantize_mx(out=q[:, half, g, :].bitcast(E4), scales=s[:, half, g, :], in_=grp[f, half, g][:])
+
+        def s_turn(key, src, on):
+            grp[key] = new_grp()
+            for i in range(2):
+                tr = ps_t.tile([P, 4, P], F32, name="tr")
+                for g in range(2):
+                    turn2(tr, 2 * g, lambda u: src(i, g, u))
+                leave(
+                    grp[key][:].bitcast(F32)[:, 512 * i : 512 * i + 512].rearrange("p (g r u) -> p g r u", g=2, u=2),
+                    tr[:].rearrange("p (g u) r -> p g r u", u=2),
+                    on,
+                )
+
+        def s_quant(key, n, q, s):
+            nc.vector.quantize_mx(
+                out=q[:, n].rearrange("p s g c -> p (s g c)").bitcast(E5),
+                scales=s[:, n].rearrange("p s g c -> p (s g c)"),
+                in_=grp[key][:],
+            )
+
+        def zm(n):
+            mask = mid.tile([P, 2, U], BF16, name="mask")
+            nc.vector.tensor_scalar(out=mask[:], in0=z_sb[n][:], scalar1=0.0, scalar2=gain[:], op0=ALU.is_gt, op1=ALU.mult)
+            w_sb = mid.tile([P, 2, 2, HALF], BF16, name="w_sb")
+            sort_mult(w_sb[:], g_sb[n][:], mask[:])
+            prod["z", n] = w_sb
+
+        def zt(n, on="ACT"):
+            s_turn(("z", n), lambda i, g, u: prod["z", n][:, u, i, 256 * g : 256 * g + 256], on)
+
+        def zq(n):
+            s_quant(("z", n), n, z2_q, z2_s)
+
+        def p1(n, i, jh, on="ACT"):
+            acc = ps_m.tile([P, HALF], F32, name="acc")
+            mx(acc, [z2_q[:, n, i, g, :] for g in range(2)], [z2_s[:, n, i, g, :] for g in range(2)],
+               [w2_q[:, jh, g, :] for g in range(2)], [w2_s[:, jh, g, :] for g in range(2)], E5, E4)
+            leave(
+                dz1[n // 2][:, 2 * (n % 2) + i, HALF * jh : HALF * jh + HALF].rearrange("p (u q r) -> p u q r", u=2, q=16),
+                acc[:].rearrange("p (q u r) -> p u q r", u=2, q=16),
+                on,
+            )
+
+        def tt(n, on="ACT"):
+            def part(i, g, u):
+                lo = HALF * g + 256 * u
+                return dz1[n // 2][:, 2 * (n % 2) + i, lo : lo + 256]
+
+            s_turn(("t", n), part, on)
+
+        def tq(n):
+            s_quant(("t", n), n, dt_q, dt_s)
+
+        def lace(key, src, on):
+            grp[key] = new_grp()
+            if on == "PE":
+                for i in range(2):
+                    tr = ps_t.tile([P, 1024], BF16, name="tr")
+                    for k in range(2):
+                        lo = 256 * i + 128 * k
+                        nc.tensor.matmul(
+                            tr[:, 512 * k : 512 * k + 512].rearrange("p (c s) -> p c s", s=4),
+                            lhsT=ident_b[:],
+                            rhs=src[:, :, lo : lo + P].rearrange("p s c -> p c s"),
+                            start=True,
+                            stop=True,
+                        )
+                    nc.scalar.copy(out=grp[key][:, 1024 * i : 1024 * i + 1024], in_=tr[:])
+            else:
+                leave(
+                    grp[key][:].rearrange("p (c i s) -> p c s i", s=4, i=4),
+                    src.rearrange("p s (c i) -> p c s i", i=4),
+                    on,
+                )
+
+        def bl(b, jh, on="DVE"):
+            lace(("b", b, jh), dz1[b][:, :, HALF * jh : HALF * jh + HALF], on)
+
+        def bq(b, jh):
+            nc.vector.quantize_mx(out=db_q[:, b, jh, :].bitcast(E5), scales=db_s[:, b, jh, :], in_=grp["b", b, jh][:])
+
+        def hl(b, ih, on="DVE"):
+            lace(("h", b, ih), h_sb[b, ih][:], on)
+
+        def hq(b, ih):
+            nc.vector.quantize_mx(out=h_q[:, b, ih, :].bitcast(E4), scales=h_s[:, b, ih, :], in_=grp["h", b, ih][:])
+
+        def p3(it, on=("DVE", "DVE")):
+            c, a = it // 2, it % 2
+            res = outs.tile([P, U], F32, name="res")
+            lo = P * (it % 4)
+            for jh in range(2):
+                acc = ps_m.tile([P, HALF], F32, name="acc")
+                mx(acc, [h_q[:, b, it // 4, lo : lo + P] for b in range(2)], [h_s[:, b, it // 4, lo : lo + P] for b in range(2)],
+                   [db_q[:, b, jh, :] for b in range(2)], [db_s[:, b, jh, :] for b in range(2)], E4, E5)
+                cols = slice(HALF * jh, HALF * jh + HALF)
+                unsorted = acc[:].rearrange("p (u q r) -> p q u r", u=2, q=16)
+                if on[jh] == "DVE":
+                    nc.vector.tensor_tensor(
+                        out=res[:, cols].rearrange("p (q u r) -> p q u r", u=2, q=16),
+                        in0=unsorted,
+                        in1=m_sb[1, c][:, a, cols].rearrange("p (q u r) -> p q u r", u=2, q=16),
+                        op=ALU.mult,
+                    )
+                else:
+                    plain = mid.tile([P, HALF], F32, name="plain")
+                    nc.scalar.copy(out=plain[:].rearrange("p (q u r) -> p q u r", u=2, q=16), in_=unsorted)
+                    nc.gpsimd.tensor_tensor(out=res[:, cols], in0=plain[:], in1=m_sb[1, c][:, a, cols], op=ALU.mult)
+            nc.sync.dma_start(out=out_1_v[it], in_=res[:])
+
+        def p2(half, n, on=("ACT", "ACT")):
+            b, s0 = n // 2, 2 * (n % 2)
+            res = outs.tile([P, 2, HALF], F32, name="res")
+            for i in range(2):
+                acc = ps_m.tile([P, HALF], F32, name="acc")
+                mx(acc, [dt_q[:, n, i, g, :] for g in range(2)], [dt_s[:, n, i, g, :] for g in range(2)],
+                   [w1_q[:, half, g, :] for g in range(2)], [w1_s[:, half, g, :] for g in range(2)], E5, E4)
+                leave(res[:, i, :], acc[:], on[i])
+            nc.sync.dma_start(out=out_0_v[b][:, s0 : s0 + 2, HALF * half : HALF * half + HALF], in_=res[:])
+
+        def ld(kind, i):
+            if kind == "w":
+                if i == 0:
+                    for a in range(2):
+                        k_sb[2, 0, a] = load(raw4, "k_sb", [1, U], BF16, k2_v[0][:, a : a + 1, :])
+                        m_sb[2, 0, a] = load(raw4, "m_sb", [1, U], BF16, m2_v[0][:, a : a + 1, :])
+                else:
+                    k_sb[2, i] = load(raw4, "k_sb", [2, U], BF16, k2_v[i])
+                    m_sb[2, i] = load(raw4, "m_sb", [2, U], BF16, m2_v[i])
+            elif kind == "z":
+                b, s0 = i // 2, 2 * (i % 2)
+                z_sb[i] = load(raw8, "z_sb", [2, U], F32, z_v[b][:, s0 : s0 + 2, :])
+                g_sb[i] = load(raw4, "g_sb", [2, U], BF16, g_v[b][:, s0 : s0 + 2, :])
+            elif kind == "h":
+                for ih in range(2):
+                    h_sb[i, ih] = load(raw_h, "h_sb", [4, HALF], BF16, h_v[i][:, :, HALF * ih : HALF * ih + HALF])
+            elif kind == "m":
+                m_sb[1, i] = load(keep_m, "m1_sb", [2, U], BF16, m1_v[i])
+            else:
+                k_sb[1, i] = load(raw4, "k_sb", [2, U], BF16, k1_v[i])
+
+        ld("h", 0)
+        nc.scalar.dma_start(out=gain_raw[:], in_=scaling.partition_broadcast(P))
+        ld("h", 1)
+        ld("z", 0)
+        ld("w", 0)
+        ld("w", 1)
+        ld("z", 1)
+        ld("w", 3)
+        ld("w", 2)
+        ld("z", 2)
+        ld("z", 3)
+        ld("m", 2)
+        ld("k", 0)
+        ld("m", 0)
+        ld("k", 1)
+        ld("m", 1)
+        ld("m", 3)
+        ld("k", 3)
+        ld("k", 2)
+        with tc.manual_schedule():
+            hl(1, 1)
+            hl(0, 1, "ACT")
+            hq(1, 1)
+            hl(1, 0, "ACT")
+            nc.vector.tensor_copy(out=gain[:], in_=gain_raw[:])
+            zm(0)
+            hl(0, 0, "ACT")
+            wm(2, 0)
+            zt(0, "DVE")
+            hq(0, 1)
+            zq(0)
+            wm(2, 1)
+            hq(1, 0)
+            wt(2, 1)
+            wt(2, 0)
+            zm(1)
+            wq(2, 0)
+            hq(0, 0)
+            zt(1)
+            p1(0, 1, 0)
+            zq(1)
+            p1(1, 1, 0)
+            wm(2, 3)
+            wm(2, 2)
+            wt(2, 3)
+            p1(1, 0, 0)
+            p1(0, 0, 0)
+            wt(2, 2)
+            zm(2)
+            wq(2, 1)
+            zt(2)
+            p1(0, 1, 1)
+            p1(0, 0, 1)
+            p1(1, 0, 1)
+            p1(1, 1, 1)
+            zm(3)
+            zt(3)
+            zq(2)
+            tt(1)
+            bl(0, 0)
+            wm(1, 0)
+            zq(3)
+            p1(2, 1, 1)
+            p1(2, 0, 1)
+            tq(1)
+            p1(2, 1, 0)
+            tt(0)
+            wm(1, 1)
+            p1(2, 0, 0)
+            wt(1, 0, "DVE")
+            wt(1, 1)
+            tt(2)
+            wm(1, 3)
+            p1(3, 1, 0)
+            bq(0, 0)
+            wt(1, 3)
+            wm(1, 2)
+            wq(1, 0)
+            tq(0)
+            p1(3, 1, 1)
+            wt(1, 2)
+            p1(3, 0, 0)
+            wq(1, 1)
+            bl(1, 0)
+            p1(3, 0, 1)
+            p2(0, 0)
+            p2(1, 0)
+            tq(2)
+            p2(0, 1, ("DVE", "ACT"))
+            bl(1, 1)
+            bq(1, 0)
+            bq(1, 1)
+            p2(1, 1, ("ACT", "DVE"))
+            bl(0, 1, "ACT")
+            p2(0, 2, ("DVE", "ACT"))
+            p2(1, 2)
+            tt(3)
+            bq(0, 1)
+            p3(2)
+            p3(1)
+            tq(3)
+            p3(4)
+            p2(1, 3, ("ACT", "DVE"))
+            p2(0, 3, ("ACT", "DVE"))
+            p3(0)
+            p3(7)
+            p3(5)
+            p3(6)
+            p3(3)

@@ -22,24 +22,25 @@ def tile_sparsefactorisationdense_pa_v_kernel(
     tc, h0, k1, k2, m1, m2, scaling, bias, z, grad_out, out_0, out_1
 ):
     nc = tc.nc
-    k1_v = k1.rearrange("(c a p) w -> c p a w", a=2, p=P)
-    k2_v = k2.rearrange("(c a p) w -> c p a w", a=2, p=P)
-    m1_v = m1.rearrange("(c a p) w -> c p a w", a=2, p=P)
-    m2_v = m2.rearrange("(c a p) w -> c p a w", a=2, p=P)
+    k1_v = k1.rearrange("(c p a) w -> c p a w", a=4, p=P)
+    k2_v = k2.rearrange("(c p a) w -> c p a w", a=2, p=P)
+    m1_v = m1.rearrange("(c p a) w -> c p a w", a=4, p=P)
+    m2_v = m2.rearrange("(c p a) w -> c p a w", a=2, p=P)
     z_v = z.rearrange("(b p s) w -> b p s w", p=P, s=4)
     g_v = grad_out.rearrange("(b p s) w -> b p s w", p=P, s=4)
     h_v = h0.rearrange("(b p s) w -> b p s w", p=P, s=4)
     out_0_v = out_0.rearrange("(b p s) w -> b p s w", p=P, s=4)
-    out_1_v = out_1.rearrange("(t p) w -> t p w", p=P)
+    out_1_v = out_1.rearrange("(c p a) w -> c p a w", a=4, p=P)
 
     with ExitStack() as ctx:
         const = ctx.enter_context(tc.tile_pool(name="const", bufs=1))
         raw8 = ctx.enter_context(tc.tile_pool(name="raw8", bufs=3))
-        raw_h = ctx.enter_context(tc.tile_pool(name="raw_h", bufs=4))
-        raw4 = ctx.enter_context(tc.tile_pool(name="raw4", bufs=3))
-        keep_m = ctx.enter_context(tc.tile_pool(name="keep_m", bufs=4))
+        plains = ctx.enter_context(tc.tile_pool(name="plains", bufs=2))
+        raw_h = ctx.enter_context(tc.tile_pool(name="raw_h", bufs=3))
+        raw4 = ctx.enter_context(tc.tile_pool(name="raw4", bufs=8))
+        mask_pool = ctx.enter_context(tc.tile_pool(name="masks", bufs=1))
         mid = ctx.enter_context(tc.tile_pool(name="mid", bufs=2))
-        grps = ctx.enter_context(tc.tile_pool(name="grps", bufs=6))
+        grps = ctx.enter_context(tc.tile_pool(name="grps", bufs=4))
         keep = ctx.enter_context(tc.tile_pool(name="keep", bufs=1))
         outs = ctx.enter_context(tc.tile_pool(name="outs", bufs=6))
         ps_t = ctx.enter_context(tc.psum_pool(name="ps_t", bufs=3))
@@ -47,8 +48,6 @@ def tile_sparsefactorisationdense_pa_v_kernel(
 
         ident = const.tile([P, P], F32, name="ident")
         make_identity(nc, ident[:])
-        ident_b = const.tile([P, P], BF16, name="ident_b")
-        make_identity(nc, ident_b[:])
         gain_raw = const.tile([P, 1], BF16, name="gain_raw")
         gain = const.tile([P, 1], F32, name="gain")
 
@@ -61,13 +60,12 @@ def tile_sparsefactorisationdense_pa_v_kernel(
         w2_q, w2_s = codes("w2", [2, 2, HALF])
         w1_q, w1_s = codes("w1", [2, 2, HALF])
         z2_q, z2_s = codes("z2", [4, 2, 2, P])
-        dt_q, dt_s = codes("dt", [4, 2, 2, P])
         db_q, db_s = codes("db", [2, 2, HALF])
         h_q, h_s = codes("h", [2, 2, HALF])
         dz1 = [keep.tile([P, 4, U], BF16, align_bytes=64, name="dz1_%d" % b) for b in range(2)]
 
-        def new_grp():
-            return grps.tile([P, 2048], BF16, align_bytes=64, name="grp")
+        def new_grp(width):
+            return grps.tile([P, width], BF16, align_bytes=64, name="grp")
 
         def load(pool, name, shape, dtype, src):
             t = pool.tile([P] + shape, dtype, name=name)
@@ -109,8 +107,9 @@ def tile_sparsefactorisationdense_pa_v_kernel(
         codes_of = {1: (w1_q, w1_s), 2: (w2_q, w2_s)}
 
         def wm(f, c):
-            w_sb = mid.tile([P, 2, 2, HALF], BF16, name="w_sb")
-            if (f, c, 0) in k_sb:
+            rows = 2 if f == 2 else 4
+            w_sb = mid.tile([P, 2, rows, HALF], BF16, name="w_sb")
+            if f == 2 and c == 0:
                 for a in range(2):
                     sort_mult(w_sb[:, :, a : a + 1, :], k_sb[f, c, a][:], m_sb[f, c, a][:])
             else:
@@ -118,55 +117,64 @@ def tile_sparsefactorisationdense_pa_v_kernel(
             prod["w", f, c] = w_sb
 
         def wt(f, c, on="ACT"):
+            half = c // 2
+            w_sb, a0 = (prod["w", 2, c], 0) if f == 2 else (prod["w", 1, half], 2 * (c % 2))
+            if (f, half) not in grp:
+                grp[f, half] = new_grp(4096)
             for g in range(2):
-                if (f, c // 2, g) not in grp:
-                    grp[f, c // 2, g] = new_grp()
                 tr = ps_t.tile([P, 4, P], F32, name="tr")
                 for a in range(2):
-                    turn2(tr, 2 * a, lambda u: prod["w", f, c][:, u, a, 256 * g : 256 * g + 256])
-                lo = 512 * (c % 2)
-                leave(
-                    grp[f, c // 2, g][:].bitcast(F32)[:, lo : lo + 512].rearrange("p (a r u) -> p a r u", a=2, u=2),
-                    tr[:].rearrange("p (a u) r -> p a r u", u=2),
-                    on,
-                )
+                    turn2(tr, 2 * a, lambda u: w_sb[:, u, a0 + a, 256 * g : 256 * g + 256])
+                words = grp[f, half][:].bitcast(F32)[:, 1024 * g : 1024 * g + 1024]
+                if f == 2:
+                    lo = 512 * (c % 2)
+                    dst = words[:, lo : lo + 512].rearrange("p (r a u) -> p r a u", a=2, u=2)
+                else:
+                    dst = words.rearrange("p (r a u) -> p r a u", a=4, u=2)[:, :, a0 : a0 + 2, :]
+                leave(dst, tr[:].rearrange("p (a u) r -> p r a u", u=2), on)
 
         def wq(f, half):
             q, s = codes_of[f]
-            for g in range(2):
-                nc.vector.quantize_mx(out=q[:, half, g, :].bitcast(E4), scales=s[:, half, g, :], in_=grp[f, half, g][:])
+            nc.vector.quantize_mx(
+                out=q[:, half].rearrange("p g c -> p (g c)").bitcast(E4),
+                scales=s[:, half].rearrange("p g c -> p (g c)"),
+                in_=grp[f, half][:],
+            )
 
-        def s_turn(key, src, on):
-            grp[key] = new_grp()
+        def s_turn(dst, src, on):
             for i in range(2):
                 tr = ps_t.tile([P, 4, P], F32, name="tr")
                 for g in range(2):
                     turn2(tr, 2 * g, lambda u: src(i, g, u))
                 leave(
-                    grp[key][:].bitcast(F32)[:, 512 * i : 512 * i + 512].rearrange("p (g r u) -> p g r u", g=2, u=2),
+                    dst.bitcast(F32)[:, 512 * i : 512 * i + 512].rearrange("p (g r u) -> p g r u", g=2, u=2),
                     tr[:].rearrange("p (g u) r -> p g r u", u=2),
                     on,
                 )
 
-        def s_quant(key, n, q, s):
+        def s_quant(src, n0, n1):
             nc.vector.quantize_mx(
-                out=q[:, n].rearrange("p s g c -> p (s g c)").bitcast(E5),
-                scales=s[:, n].rearrange("p s g c -> p (s g c)"),
-                in_=grp[key][:],
+                out=z2_q[:, n0:n1].rearrange("p n s g c -> p (n s g c)").bitcast(E5),
+                scales=z2_s[:, n0:n1].rearrange("p n s g c -> p (n s g c)"),
+                in_=src,
             )
 
-        def zm(n):
-            mask = mid.tile([P, 2, U], BF16, name="mask")
+        def zs(n):
+            mask = mask_pool.tile([P, 2, U], BF16, name="mask")
             nc.vector.tensor_scalar(out=mask[:], in0=z_sb[n][:], scalar1=0.0, scalar2=gain[:], op0=ALU.is_gt, op1=ALU.mult)
+            prod["mask", n] = mask
+
+        def zm(n):
             w_sb = mid.tile([P, 2, 2, HALF], BF16, name="w_sb")
-            sort_mult(w_sb[:], g_sb[n][:], mask[:])
+            sort_mult(w_sb[:], g_sb[n][:], prod["mask", n][:])
             prod["z", n] = w_sb
 
         def zt(n, on="ACT"):
-            s_turn(("z", n), lambda i, g, u: prod["z", n][:, u, i, 256 * g : 256 * g + 256], on)
+            grp["z", n] = mid.tile([P, 2048], BF16, align_bytes=64, name="gz")
+            s_turn(grp["z", n][:], lambda i, g, u: prod["z", n][:, u, i, 256 * g : 256 * g + 256], on)
 
         def zq(n):
-            s_quant(("z", n), n, z2_q, z2_s)
+            s_quant(grp["z", n][:], n, n + 1)
 
         def p1(n, i, jh, on="ACT"):
             acc = ps_m.tile([P, HALF], F32, name="acc")
@@ -183,52 +191,53 @@ def tile_sparsefactorisationdense_pa_v_kernel(
                 lo = HALF * g + 256 * u
                 return dz1[n // 2][:, 2 * (n % 2) + i, lo : lo + 256]
 
-            s_turn(("t", n), part, on)
+            if ("t", n // 2) not in grp:
+                grp["t", n // 2] = new_grp(4096)
+            lo = 2048 * (n % 2)
+            s_turn(grp["t", n // 2][:, lo : lo + 2048], part, on)
 
-        def tq(n):
-            s_quant(("t", n), n, dt_q, dt_s)
-
-        def lace(key, src, on):
-            grp[key] = new_grp()
-            if on == "PE":
-                for i in range(2):
-                    tr = ps_t.tile([P, 1024], BF16, name="tr")
-                    for k in range(2):
-                        lo = 256 * i + 128 * k
-                        nc.tensor.matmul(
-                            tr[:, 512 * k : 512 * k + 512].rearrange("p (c s) -> p c s", s=4),
-                            lhsT=ident_b[:],
-                            rhs=src[:, :, lo : lo + P].rearrange("p s c -> p c s"),
-                            start=True,
-                            stop=True,
-                        )
-                    nc.scalar.copy(out=grp[key][:, 1024 * i : 1024 * i + 1024], in_=tr[:])
-            else:
-                leave(
-                    grp[key][:].rearrange("p (c i s) -> p c s i", s=4, i=4),
-                    src.rearrange("p s (c i) -> p c s i", i=4),
-                    on,
-                )
+        def tq(b):
+            s_quant(grp["t", b][:], 2 * b, 2 * b + 2)
 
         def bl(b, jh, on="DVE"):
-            lace(("b", b, jh), dz1[b][:, :, HALF * jh : HALF * jh + HALF], on)
+            if ("b", b) not in grp:
+                grp["b", b] = new_grp(4096)
+            leave(
+                grp["b", b][:, 2048 * jh : 2048 * jh + 2048].rearrange("p (c i s) -> p c s i", s=4, i=4),
+                dz1[b][:, :, HALF * jh : HALF * jh + HALF].rearrange("p s (c i) -> p c s i", i=4),
+                on,
+            )
 
-        def bq(b, jh):
-            nc.vector.quantize_mx(out=db_q[:, b, jh, :].bitcast(E5), scales=db_s[:, b, jh, :], in_=grp["b", b, jh][:])
+        def bq(b):
+            nc.vector.quantize_mx(
+                out=db_q[:, b].rearrange("p h c -> p (h c)").bitcast(E5),
+                scales=db_s[:, b].rearrange("p h c -> p (h c)"),
+                in_=grp["b", b][:],
+            )
 
         def hl(b, ih, on="DVE"):
-            lace(("h", b, ih), h_sb[b, ih][:], on)
+            if ("h", b) not in grp:
+                grp["h", b] = new_grp(4096)
+            leave(
+                grp["h", b][:, 2048 * ih : 2048 * ih + 2048].rearrange("p (a c s) -> p a c s", a=4, s=4),
+                h_sb[b][:, :, HALF * ih : HALF * ih + HALF].rearrange("p s (c a) -> p a c s", a=4),
+                on,
+            )
 
-        def hq(b, ih):
-            nc.vector.quantize_mx(out=h_q[:, b, ih, :].bitcast(E4), scales=h_s[:, b, ih, :], in_=grp["h", b, ih][:])
+        def hq(b):
+            nc.vector.quantize_mx(
+                out=h_q[:, b].rearrange("p h c -> p (h c)").bitcast(E4),
+                scales=h_s[:, b].rearrange("p h c -> p (h c)"),
+                in_=grp["h", b][:],
+            )
 
         def p3(it, on=("DVE", "DVE")):
-            c, a = it // 2, it % 2
+            half, a = it // 4, it % 4
             res = outs.tile([P, U], F32, name="res")
-            lo = P * (it % 4)
+            lo = P * a
             for jh in range(2):
                 acc = ps_m.tile([P, HALF], F32, name="acc")
-                mx(acc, [h_q[:, b, it // 4, lo : lo + P] for b in range(2)], [h_s[:, b, it // 4, lo : lo + P] for b in range(2)],
+                mx(acc, [h_q[:, b, half, lo : lo + P] for b in range(2)], [h_s[:, b, half, lo : lo + P] for b in range(2)],
                    [db_q[:, b, jh, :] for b in range(2)], [db_s[:, b, jh, :] for b in range(2)], E4, E5)
                 cols = slice(HALF * jh, HALF * jh + HALF)
                 unsorted = acc[:].rearrange("p (u q r) -> p q u r", u=2, q=16)
@@ -236,21 +245,21 @@ def tile_sparsefactorisationdense_pa_v_kernel(
                     nc.vector.tensor_tensor(
                         out=res[:, cols].rearrange("p (q u r) -> p q u r", u=2, q=16),
                         in0=unsorted,
-                        in1=m_sb[1, c][:, a, cols].rearrange("p (q u r) -> p q u r", u=2, q=16),
+                        in1=m_sb[1, half][:, a, cols].rearrange("p (q u r) -> p q u r", u=2, q=16),
                         op=ALU.mult,
                     )
                 else:
-                    plain = mid.tile([P, HALF], F32, name="plain")
+                    plain = plains.tile([P, HALF], F32, name="plain")
                     nc.scalar.copy(out=plain[:].rearrange("p (q u r) -> p q u r", u=2, q=16), in_=unsorted)
-                    nc.gpsimd.tensor_tensor(out=res[:, cols], in0=plain[:], in1=m_sb[1, c][:, a, cols], op=ALU.mult)
-            nc.sync.dma_start(out=out_1_v[it], in_=res[:])
+                    nc.gpsimd.tensor_tensor(out=res[:, cols], in0=plain[:], in1=m_sb[1, half][:, a, cols], op=ALU.mult)
+            nc.sync.dma_start(out=out_1_v[half][:, a, :], in_=res[:])
 
         def p2(half, n, on=("ACT", "ACT")):
             b, s0 = n // 2, 2 * (n % 2)
             res = outs.tile([P, 2, HALF], F32, name="res")
             for i in range(2):
                 acc = ps_m.tile([P, HALF], F32, name="acc")
-                mx(acc, [dt_q[:, n, i, g, :] for g in range(2)], [dt_s[:, n, i, g, :] for g in range(2)],
+                mx(acc, [z2_q[:, n, i, g, :] for g in range(2)], [z2_s[:, n, i, g, :] for g in range(2)],
                    [w1_q[:, half, g, :] for g in range(2)], [w1_s[:, half, g, :] for g in range(2)], E5, E4)
                 leave(res[:, i, :], acc[:], on[i])
             nc.sync.dma_start(out=out_0_v[b][:, s0 : s0 + 2, HALF * half : HALF * half + HALF], in_=res[:])
@@ -259,129 +268,120 @@ def tile_sparsefactorisationdense_pa_v_kernel(
             if kind == "w":
                 if i == 0:
                     for a in range(2):
-                        k_sb[2, 0, a] = load(raw4, "k_sb", [1, U], BF16, k2_v[0][:, a : a + 1, :])
-                        m_sb[2, 0, a] = load(raw4, "m_sb", [1, U], BF16, m2_v[0][:, a : a + 1, :])
+                        k_sb[2, 0, a] = load(raw4, "r4", [1, U], BF16, k2_v[0][:, a : a + 1, :])
+                        m_sb[2, 0, a] = load(raw4, "r4", [1, U], BF16, m2_v[0][:, a : a + 1, :])
                 else:
-                    k_sb[2, i] = load(raw4, "k_sb", [2, U], BF16, k2_v[i])
-                    m_sb[2, i] = load(raw4, "m_sb", [2, U], BF16, m2_v[i])
+                    k_sb[2, i] = load(raw4, "r4", [2, U], BF16, k2_v[i])
+                    m_sb[2, i] = load(raw4, "r4", [2, U], BF16, m2_v[i])
             elif kind == "z":
                 b, s0 = i // 2, 2 * (i % 2)
-                z_sb[i] = load(raw8, "z_sb", [2, U], F32, z_v[b][:, s0 : s0 + 2, :])
-                g_sb[i] = load(raw4, "g_sb", [2, U], BF16, g_v[b][:, s0 : s0 + 2, :])
+                z_sb[i] = load(raw8, "r8", [2, U], F32, z_v[b][:, s0 : s0 + 2, :])
+                g_sb[i] = load(raw4, "r4", [2, U], BF16, g_v[b][:, s0 : s0 + 2, :])
             elif kind == "h":
-                for ih in range(2):
-                    h_sb[i, ih] = load(raw_h, "h_sb", [4, HALF], BF16, h_v[i][:, :, HALF * ih : HALF * ih + HALF])
+                h_sb[i] = load(raw_h, "hm", [4, U], BF16, h_v[i])
             elif kind == "m":
-                m_sb[1, i] = load(keep_m, "m1_sb", [2, U], BF16, m1_v[i])
+                m_sb[1, i] = load(raw_h, "hm", [4, U], BF16, m1_v[i])
             else:
-                k_sb[1, i] = load(raw4, "k_sb", [2, U], BF16, k1_v[i])
+                k_sb[1, i] = load(raw8, "r8", [4, U], BF16, k1_v[i])
 
         ld("h", 0)
         nc.scalar.dma_start(out=gain_raw[:], in_=scaling.partition_broadcast(P))
-        ld("h", 1)
+        ld("w", 2)
         ld("z", 0)
-        ld("w", 0)
         ld("w", 1)
+        ld("w", 0)
         ld("z", 1)
         ld("w", 3)
-        ld("w", 2)
-        ld("z", 2)
-        ld("z", 3)
-        ld("m", 2)
         ld("k", 0)
         ld("m", 0)
-        ld("k", 1)
         ld("m", 1)
-        ld("m", 3)
-        ld("k", 3)
-        ld("k", 2)
+        ld("k", 1)
+        ld("z", 2)
+        ld("z", 3)
+        ld("h", 1)
         with tc.manual_schedule():
-            hl(1, 1)
             hl(0, 1, "ACT")
-            hq(1, 1)
-            hl(1, 0, "ACT")
-            nc.vector.tensor_copy(out=gain[:], in_=gain_raw[:])
-            zm(0)
             hl(0, 0, "ACT")
-            wm(2, 0)
+            wm(2, 2)
+            nc.vector.tensor_copy(out=gain[:], in_=gain_raw[:])
+            zs(0)
+            zm(0)
+            wt(2, 2)
             zt(0, "DVE")
-            hq(0, 1)
             zq(0)
+            wm(2, 0)
             wm(2, 1)
-            hq(1, 0)
+            hq(0)
             wt(2, 1)
             wt(2, 0)
+            zs(1)
             zm(1)
-            wq(2, 0)
-            hq(0, 0)
-            zt(1)
-            p1(0, 1, 0)
-            zq(1)
-            p1(1, 1, 0)
             wm(2, 3)
-            wm(2, 2)
+            zt(1)
             wt(2, 3)
-            p1(1, 0, 0)
+            wq(2, 0)
+            zq(1)
             p1(0, 0, 0)
-            wt(2, 2)
-            zm(2)
             wq(2, 1)
-            zt(2)
-            p1(0, 1, 1)
-            p1(0, 0, 1)
-            p1(1, 0, 1)
+            p1(0, 1, 0)
+            p1(1, 1, 0)
             p1(1, 1, 1)
-            zm(3)
-            zt(3)
-            zq(2)
-            tt(1)
-            bl(0, 0)
             wm(1, 0)
-            zq(3)
-            p1(2, 1, 1)
-            p1(2, 0, 1)
-            tq(1)
-            p1(2, 1, 0)
-            tt(0)
-            wm(1, 1)
-            p1(2, 0, 0)
-            wt(1, 0, "DVE")
+            p1(0, 1, 1, "DVE")
+            p1(1, 0, 0)
+            p1(0, 0, 1)
+            bl(0, 0)
             wt(1, 1)
-            tt(2)
-            wm(1, 3)
-            p1(3, 1, 0)
-            bq(0, 0)
-            wt(1, 3)
-            wm(1, 2)
-            wq(1, 0)
-            tq(0)
-            p1(3, 1, 1)
-            wt(1, 2)
-            p1(3, 0, 0)
-            wq(1, 1)
-            bl(1, 0)
-            p1(3, 0, 1)
-            p2(0, 0)
-            p2(1, 0)
-            tq(2)
-            p2(0, 1, ("DVE", "ACT"))
-            bl(1, 1)
-            bq(1, 0)
-            bq(1, 1)
-            p2(1, 1, ("ACT", "DVE"))
+            p1(1, 0, 1, "DVE")
+            wm(1, 1)
+            zs(2)
+            wt(1, 0)
             bl(0, 1, "ACT")
-            p2(0, 2, ("DVE", "ACT"))
-            p2(1, 2)
+            wt(1, 3)
+            tt(0)
+            zm(2)
+            wt(1, 2)
+            bq(0)
+            zs(3)
+            zt(2)
+            zm(3)
+            zq(2)
+            hl(1, 0)
+            tt(1)
+            zt(3)
+            p1(2, 0, 1)
+            p1(2, 1, 0)
+            p1(2, 0, 0)
+            zq(3)
+            tq(0)
+            p1(2, 1, 1)
+            wq(1, 1)
+            wq(1, 0)
+            p1(3, 1, 0)
+            p1(3, 0, 0)
+            p1(3, 1, 1)
+            tt(2)
+            p1(3, 0, 1, "DVE")
+            p2(1, 0, ("DVE", "ACT"))
+            bl(1, 0)
             tt(3)
-            bq(0, 1)
-            p3(2)
+            p2(1, 1, ("DVE", "ACT"))
+            tq(1)
+            p2(0, 1)
+            p2(0, 0)
+            p2(0, 3)
+            p2(1, 3)
+            hl(1, 1)
+            p2(1, 2)
+            bl(1, 1)
+            hq(1)
+            bq(1)
+            p2(0, 2)
             p3(1)
-            tq(3)
-            p3(4)
-            p2(1, 3, ("ACT", "DVE"))
-            p2(0, 3, ("ACT", "DVE"))
-            p3(0)
-            p3(7)
-            p3(5)
+            p3(4, ("ACT", "DVE"))
             p3(6)
+            p3(7)
+            p3(0)
+            p3(2)
+            p3(5)
             p3(3)

@@ -37,17 +37,20 @@ def tile_sparsefactorisationdense_pa_v_kernel(
         raw8 = ctx.enter_context(tc.tile_pool(name="raw8", bufs=3))
         plains = ctx.enter_context(tc.tile_pool(name="plains", bufs=2))
         raw_h = ctx.enter_context(tc.tile_pool(name="raw_h", bufs=3))
-        raw4 = ctx.enter_context(tc.tile_pool(name="raw4", bufs=8))
+        raw4 = ctx.enter_context(tc.tile_pool(name="raw4", bufs=14))
         mask_pool = ctx.enter_context(tc.tile_pool(name="masks", bufs=1))
         mid = ctx.enter_context(tc.tile_pool(name="mid", bufs=2))
-        grps = ctx.enter_context(tc.tile_pool(name="grps", bufs=4))
+        grps = ctx.enter_context(tc.tile_pool(name="grps", bufs=3))
         keep = ctx.enter_context(tc.tile_pool(name="keep", bufs=1))
-        outs = ctx.enter_context(tc.tile_pool(name="outs", bufs=6))
         ps_t = ctx.enter_context(tc.psum_pool(name="ps_t", bufs=3))
         ps_m = ctx.enter_context(tc.psum_pool(name="ps_m", bufs=5))
 
         ident = const.tile([P, P], F32, name="ident")
         make_identity(nc, ident[:])
+        ident_b = const.tile([P, P], BF16, name="ident_b")
+        make_identity(nc, ident_b[:])
+        blank = const.tile([P, HALF], BF16, name="blank")
+        nc.gpsimd.memset(blank[:], 0.0)
         gain_raw = const.tile([P, 1], BF16, name="gain_raw")
         gain = const.tile([P, 1], F32, name="gain")
 
@@ -116,7 +119,7 @@ def tile_sparsefactorisationdense_pa_v_kernel(
                 sort_mult(w_sb[:], k_sb[f, c][:], m_sb[f, c][:])
             prod["w", f, c] = w_sb
 
-        def wt(f, c, on="ACT"):
+        def wt(f, c, on=("ACT", "ACT")):
             half = c // 2
             w_sb, a0 = (prod["w", 2, c], 0) if f == 2 else (prod["w", 1, half], 2 * (c % 2))
             if (f, half) not in grp:
@@ -131,7 +134,7 @@ def tile_sparsefactorisationdense_pa_v_kernel(
                     dst = words[:, lo : lo + 512].rearrange("p (r a u) -> p r a u", a=2, u=2)
                 else:
                     dst = words.rearrange("p (r a u) -> p r a u", a=4, u=2)[:, :, a0 : a0 + 2, :]
-                leave(dst, tr[:].rearrange("p (a u) r -> p r a u", u=2), on)
+                leave(dst, tr[:].rearrange("p (a u) r -> p r a u", u=2), on[g])
 
         def wq(f, half):
             q, s = codes_of[f]
@@ -149,7 +152,7 @@ def tile_sparsefactorisationdense_pa_v_kernel(
                 leave(
                     dst.bitcast(F32)[:, 512 * i : 512 * i + 512].rearrange("p (g r u) -> p g r u", g=2, u=2),
                     tr[:].rearrange("p (g u) r -> p g r u", u=2),
-                    on,
+                    on[i],
                 )
 
         def s_quant(src, n0, n1):
@@ -169,7 +172,7 @@ def tile_sparsefactorisationdense_pa_v_kernel(
             sort_mult(w_sb[:], g_sb[n][:], prod["mask", n][:])
             prod["z", n] = w_sb
 
-        def zt(n, on="ACT"):
+        def zt(n, on=("ACT", "ACT")):
             grp["z", n] = mid.tile([P, 2048], BF16, align_bytes=64, name="gz")
             s_turn(grp["z", n][:], lambda i, g, u: prod["z", n][:, u, i, 256 * g : 256 * g + 256], on)
 
@@ -186,7 +189,7 @@ def tile_sparsefactorisationdense_pa_v_kernel(
                 on,
             )
 
-        def tt(n, on="ACT"):
+        def tt(n, on=("ACT", "ACT")):
             def part(i, g, u):
                 lo = HALF * g + 256 * u
                 return dz1[n // 2][:, 2 * (n % 2) + i, lo : lo + 256]
@@ -199,30 +202,43 @@ def tile_sparsefactorisationdense_pa_v_kernel(
         def tq(b):
             s_quant(grp["t", b][:], 2 * b, 2 * b + 2)
 
-        def bl(b, jh, on="DVE"):
-            if ("b", b) not in grp:
-                grp["b", b] = new_grp(4096)
-            leave(
-                grp["b", b][:, 2048 * jh : 2048 * jh + 2048].rearrange("p (c i s) -> p c s i", s=4, i=4),
-                dz1[b][:, :, HALF * jh : HALF * jh + HALF].rearrange("p s (c i) -> p c s i", i=4),
-                on,
-            )
+        def pe_lace(dst, src):
+            for i in range(2):
+                tr = ps_t.tile([P, 1024], BF16, name="tr")
+                for k in range(2):
+                    nc.tensor.matmul(
+                        tr[:, 512 * k : 512 * k + 512].rearrange("p (c s) -> p c s", s=4),
+                        lhsT=ident_b[:],
+                        rhs=src(2 * i + k),
+                        start=True,
+                        stop=True,
+                    )
+                nc.scalar.copy(out=dst[:, 1024 * i : 1024 * i + 1024], in_=tr[:])
 
-        def bq(b):
-            nc.vector.quantize_mx(
-                out=db_q[:, b].rearrange("p h c -> p (h c)").bitcast(E5),
-                scales=db_s[:, b].rearrange("p h c -> p (h c)"),
-                in_=grp["b", b][:],
-            )
+        def bl(b, jh, on="DVE"):
+            grp["b", b, jh] = mid.tile([P, 2048], BF16, align_bytes=64, name="grb")
+            src = dz1[b][:, :, HALF * jh : HALF * jh + HALF]
+            if on == "PE":
+                pe_lace(grp["b", b, jh][:], lambda c: src[:, :, P * c : P * c + P].rearrange("p s c -> p c s"))
+            else:
+                leave(
+                    grp["b", b, jh][:].rearrange("p (c i s) -> p c s i", s=4, i=4),
+                    src.rearrange("p s (c i) -> p c s i", i=4),
+                    on,
+                )
+
+        def bq(b, jh):
+            nc.vector.quantize_mx(out=db_q[:, b, jh, :].bitcast(E5), scales=db_s[:, b, jh, :], in_=grp["b", b, jh][:])
 
         def hl(b, ih, on="DVE"):
             if ("h", b) not in grp:
                 grp["h", b] = new_grp(4096)
-            leave(
-                grp["h", b][:, 2048 * ih : 2048 * ih + 2048].rearrange("p (a c s) -> p a c s", a=4, s=4),
-                h_sb[b][:, :, HALF * ih : HALF * ih + HALF].rearrange("p s (c a) -> p a c s", a=4),
-                on,
-            )
+            dst = grp["h", b][:, 2048 * ih : 2048 * ih + 2048]
+            src = h_sb[b][:, :, HALF * ih : HALF * ih + HALF].rearrange("p s (c a) -> p a c s", a=4)
+            if on == "PE":
+                pe_lace(dst, lambda a: src[:, a])
+            else:
+                leave(dst.rearrange("p (a c s) -> p a c s", a=4, s=4), src, on)
 
         def hq(b):
             nc.vector.quantize_mx(
@@ -231,38 +247,48 @@ def tile_sparsefactorisationdense_pa_v_kernel(
                 in_=grp["h", b][:],
             )
 
-        def p3(it, on=("DVE", "DVE")):
+        def p3(it, jh, on="DVE"):
             half, a = it // 4, it % 4
-            res = outs.tile([P, U], F32, name="res")
+            if ("res3", it) not in prod:
+                prod["res3", it] = raw4.tile([P, U], F32, name="r4")
+            res = prod["res3", it]
             lo = P * a
-            for jh in range(2):
-                acc = ps_m.tile([P, HALF], F32, name="acc")
-                mx(acc, [h_q[:, b, half, lo : lo + P] for b in range(2)], [h_s[:, b, half, lo : lo + P] for b in range(2)],
-                   [db_q[:, b, jh, :] for b in range(2)], [db_s[:, b, jh, :] for b in range(2)], E4, E5)
-                cols = slice(HALF * jh, HALF * jh + HALF)
-                unsorted = acc[:].rearrange("p (u q r) -> p q u r", u=2, q=16)
-                if on[jh] == "DVE":
-                    nc.vector.tensor_tensor(
-                        out=res[:, cols].rearrange("p (q u r) -> p q u r", u=2, q=16),
-                        in0=unsorted,
-                        in1=m_sb[1, half][:, a, cols].rearrange("p (q u r) -> p q u r", u=2, q=16),
-                        op=ALU.mult,
-                    )
-                else:
-                    plain = plains.tile([P, HALF], F32, name="plain")
-                    nc.scalar.copy(out=plain[:].rearrange("p (q u r) -> p q u r", u=2, q=16), in_=unsorted)
-                    nc.gpsimd.tensor_tensor(out=res[:, cols], in0=plain[:], in1=m_sb[1, half][:, a, cols], op=ALU.mult)
-            nc.sync.dma_start(out=out_1_v[half][:, a, :], in_=res[:])
+            acc = ps_m.tile([P, HALF], F32, name="acc")
+            mx(acc, [h_q[:, b, half, lo : lo + P] for b in range(2)], [h_s[:, b, half, lo : lo + P] for b in range(2)],
+               [db_q[:, b, jh, :] for b in range(2)], [db_s[:, b, jh, :] for b in range(2)], E4, E5)
+            cols = slice(HALF * jh, HALF * jh + HALF)
+            unsorted = acc[:].rearrange("p (u q r) -> p q u r", u=2, q=16)
+            if on == "DVE":
+                nc.vector.tensor_tensor(
+                    out=res[:, cols].rearrange("p (q u r) -> p q u r", u=2, q=16),
+                    in0=unsorted,
+                    in1=m_sb[1, half][:, a, cols].rearrange("p (q u r) -> p q u r", u=2, q=16),
+                    op=ALU.mult,
+                )
+            else:
+                plain = plains.tile([P, HALF], F32, name="plain")
+                nc.scalar.copy(out=plain[:].rearrange("p (q u r) -> p q u r", u=2, q=16), in_=unsorted)
+                nc.gpsimd.tensor_tensor(out=res[:, cols], in0=plain[:], in1=m_sb[1, half][:, a, cols], op=ALU.mult)
 
-        def p2(half, n, on=("ACT", "ACT")):
+        def s3(it):
+            nc.sync.dma_start(out=out_1_v[it // 4][:, it % 4, :], in_=prod["res3", it][:])
+
+        def p2(half, n, i, on="ACT"):
+            if ("res2", half, n) not in prod:
+                prod["res2", half, n] = raw4.tile([P, 2, HALF], F32, name="r4")
+            acc = ps_m.tile([P, HALF], F32, name="acc")
+            mx(acc, [z2_q[:, n, i, g, :] for g in range(2)], [z2_s[:, n, i, g, :] for g in range(2)],
+               [w1_q[:, half, g, :] for g in range(2)], [w1_s[:, half, g, :] for g in range(2)], E5, E4)
+            leave(prod["res2", half, n][:, i, :], acc[:], on)
+
+        def s2(half, n):
             b, s0 = n // 2, 2 * (n % 2)
-            res = outs.tile([P, 2, HALF], F32, name="res")
-            for i in range(2):
-                acc = ps_m.tile([P, HALF], F32, name="acc")
-                mx(acc, [z2_q[:, n, i, g, :] for g in range(2)], [z2_s[:, n, i, g, :] for g in range(2)],
-                   [w1_q[:, half, g, :] for g in range(2)], [w1_s[:, half, g, :] for g in range(2)], E5, E4)
-                leave(res[:, i, :], acc[:], on[i])
-            nc.sync.dma_start(out=out_0_v[b][:, s0 : s0 + 2, HALF * half : HALF * half + HALF], in_=res[:])
+            nc.sync.dma_start(out=out_0_v[b][:, s0 : s0 + 2, HALF * half : HALF * half + HALF], in_=prod["res2", half, n][:])
+
+        def dm(i, count):
+            acc = ps_m.tile([P, HALF], F32, name="acc")
+            for k in range(count):
+                nc.tensor.matmul(acc[:], lhsT=ident_b[:], rhs=blank[:], start=True, stop=True)
 
         def ld(kind, i):
             if kind == "w":
@@ -284,104 +310,146 @@ def tile_sparsefactorisationdense_pa_v_kernel(
             else:
                 k_sb[1, i] = load(raw8, "r8", [4, U], BF16, k1_v[i])
 
-        ld("h", 0)
-        nc.scalar.dma_start(out=gain_raw[:], in_=scaling.partition_broadcast(P))
-        ld("w", 2)
-        ld("z", 0)
         ld("w", 1)
+        nc.scalar.dma_start(out=gain_raw[:], in_=scaling.partition_broadcast(P))
         ld("w", 0)
-        ld("z", 1)
-        ld("w", 3)
-        ld("k", 0)
-        ld("m", 0)
-        ld("m", 1)
-        ld("k", 1)
         ld("z", 2)
         ld("z", 3)
+        ld("w", 3)
+        ld("w", 2)
+        ld("z", 1)
+        ld("z", 0)
         ld("h", 1)
+        ld("m", 1)
+        ld("k", 1)
+        ld("k", 0)
+        ld("m", 0)
+        ld("h", 0)
         with tc.manual_schedule():
-            hl(0, 1, "ACT")
-            hl(0, 0, "ACT")
-            wm(2, 2)
-            nc.vector.tensor_copy(out=gain[:], in_=gain_raw[:])
-            zs(0)
-            zm(0)
-            wt(2, 2)
-            zt(0, "DVE")
-            zq(0)
-            wm(2, 0)
             wm(2, 1)
-            hq(0)
-            wt(2, 1)
-            wt(2, 0)
+            dm(10, 1)
+            dm(1, 1)
+            wm(2, 0)
+            wt(2, 1, ("ACT", "DVE"))
+            wt(2, 0, ("DVE", "ACT"))
+            nc.vector.tensor_copy(out=gain[:], in_=gain_raw[:])
+            zs(2)
+            dm(4, 1)
+            zm(2)
+            wq(2, 0)
+            zt(2)
+            dm(8, 2)
+            zs(3)
+            zm(3)
+            dm(9, 2)
+            zt(3)
+            zq(2)
+            wm(2, 3)
+            p1(2, 1, 0)
+            zq(3)
+            p1(2, 0, 0)
+            wt(2, 3, ("DVE", "ACT"))
+            p1(3, 0, 0)
+            p1(3, 1, 0)
+            dm(0, 2)
+            wm(2, 2)
+            wt(2, 2)
             zs(1)
             zm(1)
-            wm(2, 3)
-            zt(1)
-            wt(2, 3)
-            wq(2, 0)
-            zq(1)
-            p1(0, 0, 0)
+            bl(1, 0, "PE")
             wq(2, 1)
-            p1(0, 1, 0)
-            p1(1, 1, 0)
-            p1(1, 1, 1)
-            wm(1, 0)
-            p1(0, 1, 1, "DVE")
-            p1(1, 0, 0)
-            p1(0, 0, 1)
-            bl(0, 0)
-            wt(1, 1)
-            p1(1, 0, 1, "DVE")
-            wm(1, 1)
-            zs(2)
-            wt(1, 0)
-            bl(0, 1, "ACT")
-            wt(1, 3)
-            tt(0)
-            zm(2)
-            wt(1, 2)
-            bq(0)
-            zs(3)
-            zt(2)
-            zm(3)
-            zq(2)
-            hl(1, 0)
-            tt(1)
-            zt(3)
-            p1(2, 0, 1)
-            p1(2, 1, 0)
-            p1(2, 0, 0)
-            zq(3)
-            tq(0)
-            p1(2, 1, 1)
-            wq(1, 1)
-            wq(1, 0)
-            p1(3, 1, 0)
-            p1(3, 0, 0)
+            dm(2, 2)
+            zt(1)
+            zs(0)
+            dm(7, 1)
             p1(3, 1, 1)
+            zq(1)
+            p1(2, 0, 1)
+            p1(2, 1, 1)
+            zm(0)
+            p1(1, 0, 1)
+            hl(1, 0)
             tt(2)
-            p1(3, 0, 1, "DVE")
-            p2(1, 0, ("DVE", "ACT"))
-            bl(1, 0)
-            tt(3)
-            p2(1, 1, ("DVE", "ACT"))
-            tq(1)
-            p2(0, 1)
-            p2(0, 0)
-            p2(0, 3)
-            p2(1, 3)
-            hl(1, 1)
-            p2(1, 2)
+            p1(3, 0, 1)
+            bq(1, 0)
+            zt(0, ("ACT", "DVE"))
             bl(1, 1)
+            zq(0)
+            p1(1, 1, 0)
+            hl(1, 1, "PE")
+            wm(1, 1)
+            p1(1, 0, 0)
             hq(1)
-            bq(1)
-            p2(0, 2)
-            p3(1)
-            p3(4, ("ACT", "DVE"))
-            p3(6)
-            p3(7)
-            p3(0)
-            p3(2)
-            p3(5)
-            p3(3)
+            tt(3)
+            p1(0, 0, 1)
+            p1(0, 0, 0)
+            p1(1, 1, 1, "DVE")
+            p1(0, 1, 1)
+            wt(1, 3)
+            wt(1, 2, ("DVE", "ACT"))
+            tq(1)
+            p1(0, 1, 0)
+            tt(1)
+            tt(0)
+            wq(1, 1)
+            p2(1, 2, 0)
+            p2(1, 3, 0)
+            wm(1, 0)
+            p2(1, 2, 1, "DVE")
+            p2(1, 3, 1)
+            tq(0)
+            wt(1, 1)
+            bl(0, 1)
+            s2(1, 2)
+            s2(1, 3)
+            wt(1, 0)
+            p2(1, 1, 0, "DVE")
+            p2(1, 0, 0)
+            p2(1, 1, 1)
+            wq(1, 0)
+            p2(1, 0, 1)
+            hl(0, 1, "PE")
+            s2(1, 1)
+            p2(0, 2, 0)
+            bq(0, 1)
+            hl(0, 0)
+            s2(1, 0)
+            bq(1, 1)
+            hq(0)
+            p2(0, 2, 1)
+            bl(0, 0)
+            s2(0, 2)
+            bq(0, 0)
+            p2(0, 0, 1)
+            p2(0, 0, 0)
+            p2(0, 3, 0)
+            p2(0, 3, 1)
+            p2(0, 1, 1)
+            p2(0, 1, 0)
+            s2(0, 0)
+            p3(0, 1)
+            s2(0, 3)
+            s2(0, 1)
+            p3(5, 1, "ACT")
+            p3(0, 0)
+            p3(2, 0, "ACT")
+            s3(0)
+            p3(5, 0)
+            p3(2, 1)
+            s3(5)
+            p3(4, 1)
+            p3(4, 0)
+            p3(7, 1)
+            s3(2)
+            p3(7, 0)
+            p3(1, 0)
+            s3(4)
+            p3(1, 1)
+            s3(7)
+            p3(3, 0)
+            p3(3, 1)
+            s3(1)
+            s3(3)
+            p3(6, 1)
+            p3(6, 0)
+            s3(6)

@@ -47,10 +47,6 @@ def tile_sparsefactorisationdense_pa_v_kernel(
 
         ident = const.tile([P, P], F32, name="ident")
         make_identity(nc, ident[:])
-        ident_b = const.tile([P, P], BF16, name="ident_b")
-        make_identity(nc, ident_b[:])
-        blank = const.tile([P, HALF], BF16, name="blank")
-        nc.gpsimd.memset(blank[:], 0.0)
         gain_raw = const.tile([P, 1], BF16, name="gain_raw")
         gain = const.tile([P, 1], F32, name="gain")
 
@@ -202,30 +198,14 @@ def tile_sparsefactorisationdense_pa_v_kernel(
         def tq(b):
             s_quant(grp["t", b][:], 2 * b, 2 * b + 2)
 
-        def pe_lace(dst, src):
-            for i in range(2):
-                tr = ps_t.tile([P, 1024], BF16, name="tr")
-                for k in range(2):
-                    nc.tensor.matmul(
-                        tr[:, 512 * k : 512 * k + 512].rearrange("p (c s) -> p c s", s=4),
-                        lhsT=ident_b[:],
-                        rhs=src(2 * i + k),
-                        start=True,
-                        stop=True,
-                    )
-                nc.scalar.copy(out=dst[:, 1024 * i : 1024 * i + 1024], in_=tr[:])
-
         def bl(b, jh, on="DVE"):
             grp["b", b, jh] = mid.tile([P, 2048], BF16, align_bytes=64, name="grb")
             src = dz1[b][:, :, HALF * jh : HALF * jh + HALF]
-            if on == "PE":
-                pe_lace(grp["b", b, jh][:], lambda c: src[:, :, P * c : P * c + P].rearrange("p s c -> p c s"))
-            else:
-                leave(
-                    grp["b", b, jh][:].rearrange("p (c i s) -> p c s i", s=4, i=4),
-                    src.rearrange("p s (c i) -> p c s i", i=4),
-                    on,
-                )
+            leave(
+                grp["b", b, jh][:].rearrange("p (c i s) -> p c s i", s=4, i=4),
+                src.rearrange("p s (c i) -> p c s i", i=4),
+                on,
+            )
 
         def bq(b, jh):
             nc.vector.quantize_mx(out=db_q[:, b, jh, :].bitcast(E5), scales=db_s[:, b, jh, :], in_=grp["b", b, jh][:])
@@ -235,10 +215,7 @@ def tile_sparsefactorisationdense_pa_v_kernel(
                 grp["h", b] = new_grp(4096)
             dst = grp["h", b][:, 2048 * ih : 2048 * ih + 2048]
             src = h_sb[b][:, :, HALF * ih : HALF * ih + HALF].rearrange("p s (c a) -> p a c s", a=4)
-            if on == "PE":
-                pe_lace(dst, lambda a: src[:, a])
-            else:
-                leave(dst.rearrange("p (a c s) -> p a c s", a=4, s=4), src, on)
+            leave(dst.rearrange("p (a c s) -> p a c s", a=4, s=4), src, on)
 
         def hq(b):
             nc.vector.quantize_mx(
@@ -285,11 +262,6 @@ def tile_sparsefactorisationdense_pa_v_kernel(
             b, s0 = n // 2, 2 * (n % 2)
             nc.sync.dma_start(out=out_0_v[b][:, s0 : s0 + 2, HALF * half : HALF * half + HALF], in_=prod["res2", half, n][:])
 
-        def dm(i, count):
-            acc = ps_m.tile([P, HALF], F32, name="acc")
-            for k in range(count):
-                nc.tensor.matmul(acc[:], lhsT=ident_b[:], rhs=blank[:], start=True, stop=True)
-
         def ld(kind, i):
             if kind == "w":
                 if i == 0:
@@ -310,146 +282,138 @@ def tile_sparsefactorisationdense_pa_v_kernel(
             else:
                 k_sb[1, i] = load(raw8, "r8", [4, U], BF16, k1_v[i])
 
-        ld("w", 1)
-        nc.scalar.dma_start(out=gain_raw[:], in_=scaling.partition_broadcast(P))
-        ld("w", 0)
-        ld("z", 2)
-        ld("z", 3)
-        ld("w", 3)
-        ld("w", 2)
-        ld("z", 1)
         ld("z", 0)
-        ld("h", 1)
+        nc.scalar.dma_start(out=gain_raw[:], in_=scaling.partition_broadcast(P))
+        ld("w", 2)
+        ld("w", 0)
+        ld("w", 3)
+        ld("w", 1)
+        ld("z", 1)
+        ld("z", 3)
+        ld("z", 2)
+        ld("h", 0)
         ld("m", 1)
         ld("k", 1)
         ld("k", 0)
         ld("m", 0)
-        ld("h", 0)
+        ld("h", 1)
         with tc.manual_schedule():
-            wm(2, 1)
-            dm(10, 1)
-            dm(1, 1)
-            wm(2, 0)
-            wt(2, 1, ("ACT", "DVE"))
-            wt(2, 0, ("DVE", "ACT"))
             nc.vector.tensor_copy(out=gain[:], in_=gain_raw[:])
-            zs(2)
-            dm(4, 1)
-            zm(2)
-            wq(2, 0)
-            zt(2)
-            dm(8, 2)
-            zs(3)
-            zm(3)
-            dm(9, 2)
-            zt(3)
-            zq(2)
-            wm(2, 3)
-            p1(2, 1, 0)
-            zq(3)
-            p1(2, 0, 0)
-            wt(2, 3, ("DVE", "ACT"))
-            p1(3, 0, 0)
-            p1(3, 1, 0)
-            dm(0, 2)
-            wm(2, 2)
-            wt(2, 2)
-            zs(1)
-            zm(1)
-            bl(1, 0, "PE")
-            wq(2, 1)
-            dm(2, 2)
-            zt(1)
             zs(0)
-            dm(7, 1)
-            p1(3, 1, 1)
-            zq(1)
-            p1(2, 0, 1)
-            p1(2, 1, 1)
             zm(0)
-            p1(1, 0, 1)
-            hl(1, 0)
-            tt(2)
-            p1(3, 0, 1)
-            bq(1, 0)
-            zt(0, ("ACT", "DVE"))
-            bl(1, 1)
+            wm(2, 2)
+            zt(0)
+            wm(2, 0)
+            wt(2, 2, ("DVE", "ACT"))
             zq(0)
-            p1(1, 1, 0)
-            hl(1, 1, "PE")
-            wm(1, 1)
-            p1(1, 0, 0)
-            hq(1)
-            tt(3)
-            p1(0, 0, 1)
-            p1(0, 0, 0)
-            p1(1, 1, 1, "DVE")
+            wm(2, 3)
+            wt(2, 0, ("DVE", "ACT"))
+            wt(2, 3)
+            wm(2, 1)
+            wt(2, 1)
+            wq(2, 1)
+            zs(1)
             p1(0, 1, 1)
-            wt(1, 3)
-            wt(1, 2, ("DVE", "ACT"))
-            tq(1)
+            zm(1)
+            p1(0, 0, 1)
+            wq(2, 0)
+            zt(1)
+            p1(0, 0, 0)
+            zs(3)
+            zq(1)
             p1(0, 1, 0)
-            tt(1)
             tt(0)
-            wq(1, 1)
-            p2(1, 2, 0)
-            p2(1, 3, 0)
-            wm(1, 0)
-            p2(1, 2, 1, "DVE")
-            p2(1, 3, 1)
-            tq(0)
-            wt(1, 1)
-            bl(0, 1)
-            s2(1, 2)
-            s2(1, 3)
-            wt(1, 0)
-            p2(1, 1, 0, "DVE")
-            p2(1, 0, 0)
-            p2(1, 1, 1)
-            wq(1, 0)
-            p2(1, 0, 1)
-            hl(0, 1, "PE")
-            s2(1, 1)
-            p2(0, 2, 0)
-            bq(0, 1)
+            zm(3)
+            p1(1, 1, 1)
+            zs(2)
+            zm(2)
+            zt(3)
+            p1(1, 1, 0, "DVE")
+            p1(1, 0, 1)
+            p1(1, 0, 0)
+            zq(3)
+            zt(2)
+            hl(0, 1)
+            bl(0, 0, "ACT")
             hl(0, 0)
-            s2(1, 0)
-            bq(1, 1)
+            p1(3, 0, 0)
+            p1(3, 1, 1)
+            zq(2)
             hq(0)
-            p2(0, 2, 1)
-            bl(0, 0)
-            s2(0, 2)
+            p1(3, 1, 0)
+            wm(1, 1)
+            tt(1)
+            p1(2, 1, 1, "DVE")
+            p1(2, 0, 1, "DVE")
+            p1(3, 0, 1)
+            p1(2, 1, 0, "DVE")
+            tq(0)
+            p1(2, 0, 0)
+            wm(1, 0)
+            wt(1, 2)
+            wt(1, 3)
+            tt(2)
+            wq(1, 1)
+            tt(3, ("ACT", "DVE"))
+            hl(1, 0, "ACT")
+            wt(1, 1)
+            p2(1, 0, 0)
+            hl(1, 1)
+            p2(1, 0, 1)
+            tq(1)
+            bl(1, 0)
+            wt(1, 0)
             bq(0, 0)
-            p2(0, 0, 1)
-            p2(0, 0, 0)
+            p2(1, 1, 0, "DVE")
+            wq(1, 0)
+            bq(1, 0)
+            s2(1, 0)
+            p2(1, 1, 1)
+            p2(1, 3, 0)
+            p2(1, 3, 1)
+            hq(1)
+            bl(0, 1)
+            bl(1, 1)
+            p2(1, 2, 1)
+            s2(1, 1)
+            p2(1, 2, 0)
+            bq(0, 1)
             p2(0, 3, 0)
             p2(0, 3, 1)
-            p2(0, 1, 1)
+            s2(1, 3)
+            p2(0, 0, 0)
+            p2(0, 0, 1)
+            s2(1, 2)
             p2(0, 1, 0)
-            s2(0, 0)
-            p3(0, 1)
+            p2(0, 1, 1)
+            bq(1, 1)
             s2(0, 3)
-            s2(0, 1)
-            p3(5, 1, "ACT")
-            p3(0, 0)
-            p3(2, 0, "ACT")
-            s3(0)
-            p3(5, 0)
-            p3(2, 1)
-            s3(5)
-            p3(4, 1)
+            s2(0, 0)
+            p2(0, 2, 1)
+            p2(0, 2, 0)
             p3(4, 0)
-            p3(7, 1)
-            s3(2)
-            p3(7, 0)
-            p3(1, 0)
-            s3(4)
-            p3(1, 1)
-            s3(7)
-            p3(3, 0)
-            p3(3, 1)
-            s3(1)
-            s3(3)
+            p3(6, 0, "ACT")
+            p3(4, 1)
             p3(6, 1)
-            p3(6, 0)
+            s2(0, 1)
+            s2(0, 2)
+            p3(3, 1)
+            p3(2, 1, "ACT")
+            p3(3, 0)
+            p3(2, 0)
+            p3(7, 0)
+            p3(0, 1, "ACT")
+            s3(4)
             s3(6)
+            p3(7, 1)
+            p3(0, 0)
+            p3(1, 1)
+            p3(1, 0)
+            s3(3)
+            p3(5, 0)
+            p3(5, 1)
+            s3(2)
+            s3(7)
+            s3(0)
+            s3(1)
+            s3(5)

@@ -47,7 +47,12 @@ def tile_sparsefactorisationdense_pa_v_kernel(
 
         ident = const.tile([P, P], F32, name="ident")
         make_identity(nc, ident[:])
-        gain_raw = const.tile([P, 1], BF16, name="gain_raw")
+        ones = const.tile([P, P], BF16, name="ones")
+        nc.gpsimd.memset(ones[:], 1.0)
+        gain_in = const.tile([P, 1], BF16, name="gain_in")
+        nc.scalar.dma_start(out=gain_in[0:1, :], in_=scaling.rearrange("(p w) -> p w", p=1))
+        gain_row = const.tile([P, 64], BF16, name="gain_row")
+        nc.gpsimd.memset(gain_row[:], 0.0)
         gain = const.tile([P, 1], F32, name="gain")
 
         def codes(name, dims):
@@ -282,9 +287,8 @@ def tile_sparsefactorisationdense_pa_v_kernel(
             else:
                 k_sb[1, i] = load(raw8, "r8", [4, U], BF16, k1_v[i])
 
-        ld("z", 0)
-        nc.scalar.dma_start(out=gain_raw[:], in_=scaling.partition_broadcast(P))
         ld("w", 2)
+        ld("z", 0)
         ld("w", 0)
         ld("w", 3)
         ld("w", 1)
@@ -298,13 +302,16 @@ def tile_sparsefactorisationdense_pa_v_kernel(
         ld("m", 0)
         ld("h", 1)
         with tc.manual_schedule():
-            nc.vector.tensor_copy(out=gain[:], in_=gain_raw[:])
-            zs(0)
-            zm(0)
+            nc.scalar.copy(out=gain_row[0:1, 0:1], in_=gain_in[0:1, :])
+            spread = ps_m.tile([P, HALF], F32, name="acc")
+            nc.tensor.matmul(spread[:, 0:64], lhsT=ones[:], rhs=gain_row[:], start=True, stop=True)
+            nc.scalar.copy(out=gain[:], in_=spread[:, 0:1])
             wm(2, 2)
+            zs(0)
+            wt(2, 2, ("ACT", "ACT"))
+            zm(0)
             zt(0)
             wm(2, 0)
-            wt(2, 2, ("DVE", "ACT"))
             zq(0)
             wm(2, 3)
             wt(2, 0, ("DVE", "ACT"))

from contextlib import ExitStack

import concourse.mybir as mybir
from concourse.masks import make_identity

FLOPS = 3 * 2 * 1024 * 1024 * 1024

F32 = mybir.dt.float32
BF16 = mybir.dt.bfloat16
U32 = mybir.dt.uint32
U8 = mybir.dt.uint8
E4 = mybir.dt.float8_e4m3fn_x4
E5 = mybir.dt.float8_e5m2_x4
ALU = mybir.AluOpType

P = 128
U = 1024
HALF = 512


def tile_sparsefactorisationdense_pa_v_kernel(
    tc, h0, k1, k2, m1, m2, scaling, bias, z, grad_out, out_0, out_1
):
    nc = tc.nc
    k1_v = k1.rearrange("(c p a) w -> c p a w", a=4, p=P)
    k2_v = k2.rearrange("(c p a) w -> c p a w", a=2, p=P)
    m1_v = m1.rearrange("(c p a) w -> c p a w", a=4, p=P)
    m2_v = m2.rearrange("(c p a) w -> c p a w", a=2, p=P)
    z_v = z.rearrange("(b p s) w -> b p s w", p=P, s=4)
    g_v = grad_out.rearrange("(b p s) w -> b p s w", p=P, s=4)
    h_v = h0.rearrange("(b p s) w -> b p s w", p=P, s=4)
    out_0_v = out_0.rearrange("(b p s) w -> b p s w", p=P, s=4)
    out_1_v = out_1.rearrange("(c p a) w -> c p a w", a=4, p=P)

    with ExitStack() as ctx:
        const = ctx.enter_context(tc.tile_pool(name="const", bufs=1))
        raw8 = ctx.enter_context(tc.tile_pool(name="raw8", bufs=3))
        plains = ctx.enter_context(tc.tile_pool(name="plains", bufs=2))
        raw_h = ctx.enter_context(tc.tile_pool(name="raw_h", bufs=3))
        raw4 = ctx.enter_context(tc.tile_pool(name="raw4", bufs=14))
        mask_pool = ctx.enter_context(tc.tile_pool(name="masks", bufs=1))
        mid = ctx.enter_context(tc.tile_pool(name="mid", bufs=2))
        grps = ctx.enter_context(tc.tile_pool(name="grps", bufs=3))
        keep = ctx.enter_context(tc.tile_pool(name="keep", bufs=1))
        ps_t = ctx.enter_context(tc.psum_pool(name="ps_t", bufs=3))
        ps_m = ctx.enter_context(tc.psum_pool(name="ps_m", bufs=5))

        ident = const.tile([P, P], F32, name="ident")
        make_identity(nc, ident[:])
        ones = const.tile([P, P], BF16, name="ones")
        nc.gpsimd.memset(ones[:], 1.0)
        gain_in = const.tile([P, 1], BF16, name="gain_in")
        nc.scalar.dma_start(out=gain_in[0:1, :], in_=scaling.rearrange("(p w) -> p w", p=1))
        gain_row = const.tile([P, 64], BF16, name="gain_row")
        nc.gpsimd.memset(gain_row[:], 0.0)
        gain = const.tile([P, 1], F32, name="gain")

        def codes(name, dims):
            return (
                keep.tile([P] + dims, U32, align_bytes=64, name=name + "_q"),
                keep.tile([P] + dims, U8, align_bytes=64, name=name + "_s"),
            )

        w2_q, w2_s = codes("w2", [2, 2, HALF])
        w1_q, w1_s = codes("w1", [2, 2, HALF])
        z2_q, z2_s = codes("z2", [4, 2, 2, P])
        db_q, db_s = codes("db", [2, 2, HALF])
        h_q, h_s = codes("h", [2, 2, HALF])
        dz1 = [keep.tile([P, 4, U], BF16, align_bytes=64, name="dz1_%d" % b) for b in range(2)]

        def new_grp(width):
            return grps.tile([P, width], BF16, align_bytes=64, name="grp")

        def load(pool, name, shape, dtype, src):
            t = pool.tile([P] + shape, dtype, name=name)
            nc.sync.dma_start(out=t[:], in_=src)
            return t

        def sort_mult(dst, a, b):
            nc.vector.tensor_tensor(
                out=dst.rearrange("p u a (q r) -> p u (a q) r", r=16),
                in0=a.rearrange("p a (q u r) -> p u (a q) r", u=2, r=16),
                in1=b.rearrange("p a (q u r) -> p u (a q) r", u=2, r=16),
                op=ALU.mult,
            )

        def leave(out, in_, on):
            if on == "DVE":
                nc.vector.tensor_copy(out=out, in_=in_)
            else:
                nc.scalar.copy(out=out, in_=in_)

        def turn2(tr, k, half):
            for u in range(2):
                nc.tensor.transpose(tr[:, k + u, :], half(u).bitcast(F32), ident[:])

        def mx(acc, lq, ls, rq, rs, ldt, rdt):
            for g in range(2):
                nc.tensor.matmul_mx(
                    out=acc[:],
                    lhsT=lq[g].bitcast(ldt),
                    lhsT_scale=ls[g],
                    rhs=rq[g].bitcast(rdt),
                    rhs_scale=rs[g],
                    start=(g == 0),
                    stop=(g == 1),
                )

        prod, grp = {}, {}
        k_sb, m_sb, z_sb, g_sb, h_sb = {}, {}, {}, {}, {}
        codes_of = {1: (w1_q, w1_s), 2: (w2_q, w2_s)}

        def wm(f, c):
            rows = 2 if f == 2 else 4
            w_sb = mid.tile([P, 2, rows, HALF], BF16, name="w_sb")
            if f == 2 and c == 0:
                for a in range(2):
                    sort_mult(w_sb[:, :, a : a + 1, :], k_sb[f, c, a][:], m_sb[f, c, a][:])
            else:
                sort_mult(w_sb[:], k_sb[f, c][:], m_sb[f, c][:])
            prod["w", f, c] = w_sb

        def wt(f, c, on=("ACT", "ACT")):
            half = c // 2
            w_sb, a0 = (prod["w", 2, c], 0) if f == 2 else (prod["w", 1, half], 2 * (c % 2))
            if (f, half) not in grp:
                grp[f, half] = new_grp(4096)
            for g in range(2):
                tr = ps_t.tile([P, 4, P], F32, name="tr")
                for a in range(2):
                    turn2(tr, 2 * a, lambda u: w_sb[:, u, a0 + a, 256 * g : 256 * g + 256])
                words = grp[f, half][:].bitcast(F32)[:, 1024 * g : 1024 * g + 1024]
                if f == 2:
                    lo = 512 * (c % 2)
                    dst = words[:, lo : lo + 512].rearrange("p (r a u) -> p r a u", a=2, u=2)
                else:
                    dst = words.rearrange("p (r a u) -> p r a u", a=4, u=2)[:, :, a0 : a0 + 2, :]
                leave(dst, tr[:].rearrange("p (a u) r -> p r a u", u=2), on[g])

        def wq(f, half):
            q, s = codes_of[f]
            nc.vector.quantize_mx(
                out=q[:, half].rearrange("p g c -> p (g c)").bitcast(E4),
                scales=s[:, half].rearrange("p g c -> p (g c)"),
                in_=grp[f, half][:],
            )

        def s_turn(dst, src, on):
            for i in range(2):
                tr = ps_t.tile([P, 4, P], F32, name="tr")
                for g in range(2):
                    turn2(tr, 2 * g, lambda u: src(i, g, u))
                leave(
                    dst.bitcast(F32)[:, 512 * i : 512 * i + 512].rearrange("p (g r u) -> p g r u", g=2, u=2),
                    tr[:].rearrange("p (g u) r -> p g r u", u=2),
                    on[i],
                )

        def s_quant(src, n0, n1):
            nc.vector.quantize_mx(
                out=z2_q[:, n0:n1].rearrange("p n s g c -> p (n s g c)").bitcast(E5),
                scales=z2_s[:, n0:n1].rearrange("p n s g c -> p (n s g c)"),
                in_=src,
            )

        def zs(n):
            mask = mask_pool.tile([P, 2, U], BF16, name="mask")
            nc.vector.tensor_scalar(out=mask[:], in0=z_sb[n][:], scalar1=0.0, scalar2=gain[:], op0=ALU.is_gt, op1=ALU.mult)
            prod["mask", n] = mask

        def zm(n):
            w_sb = mid.tile([P, 2, 2, HALF], BF16, name="w_sb")
            sort_mult(w_sb[:], g_sb[n][:], prod["mask", n][:])
            prod["z", n] = w_sb

        def zt(n, on=("ACT", "ACT")):
            grp["z", n] = mid.tile([P, 2048], BF16, align_bytes=64, name="gz")
            s_turn(grp["z", n][:], lambda i, g, u: prod["z", n][:, u, i, 256 * g : 256 * g + 256], on)

        def zq(n):
            s_quant(grp["z", n][:], n, n + 1)

        def p1(n, i, jh, on="ACT"):
            acc = ps_m.tile([P, HALF], F32, name="acc")
            mx(acc, [z2_q[:, n, i, g, :] for g in range(2)], [z2_s[:, n, i, g, :] for g in range(2)],
               [w2_q[:, jh, g, :] for g in range(2)], [w2_s[:, jh, g, :] for g in range(2)], E5, E4)
            leave(
                dz1[n // 2][:, 2 * (n % 2) + i, HALF * jh : HALF * jh + HALF].rearrange("p (u q r) -> p u q r", u=2, q=16),
                acc[:].rearrange("p (q u r) -> p u q r", u=2, q=16),
                on,
            )

        def tt(n, on=("ACT", "ACT")):
            def part(i, g, u):
                lo = HALF * g + 256 * u
                return dz1[n // 2][:, 2 * (n % 2) + i, lo : lo + 256]

            if ("t", n // 2) not in grp:
                grp["t", n // 2] = new_grp(4096)
            lo = 2048 * (n % 2)
            s_turn(grp["t", n // 2][:, lo : lo + 2048], part, on)

        def tq(b):
            s_quant(grp["t", b][:], 2 * b, 2 * b + 2)

        def bl(b, jh, on="DVE"):
            grp["b", b, jh] = mid.tile([P, 2048], BF16, align_bytes=64, name="grb")
            src = dz1[b][:, :, HALF * jh : HALF * jh + HALF]
            leave(
                grp["b", b, jh][:].rearrange("p (c i s) -> p c s i", s=4, i=4),
                src.rearrange("p s (c i) -> p c s i", i=4),
                on,
            )

        def bq(b, jh):
            nc.vector.quantize_mx(out=db_q[:, b, jh, :].bitcast(E5), scales=db_s[:, b, jh, :], in_=grp["b", b, jh][:])

        def hl(b, ih, on="DVE"):
            if ("h", b) not in grp:
                grp["h", b] = new_grp(4096)
            dst = grp["h", b][:, 2048 * ih : 2048 * ih + 2048]
            src = h_sb[b][:, :, HALF * ih : HALF * ih + HALF].rearrange("p s (c a) -> p a c s", a=4)
            leave(dst.rearrange("p (a c s) -> p a c s", a=4, s=4), src, on)

        def hq(b):
            nc.vector.quantize_mx(
                out=h_q[:, b].rearrange("p h c -> p (h c)").bitcast(E4),
                scales=h_s[:, b].rearrange("p h c -> p (h c)"),
                in_=grp["h", b][:],
            )

        def p3(it, jh, on="DVE"):
            half, a = it // 4, it % 4
            if ("res3", it) not in prod:
                prod["res3", it] = raw4.tile([P, U], F32, name="r4")
            res = prod["res3", it]
            lo = P * a
            acc = ps_m.tile([P, HALF], F32, name="acc")
            mx(acc, [h_q[:, b, half, lo : lo + P] for b in range(2)], [h_s[:, b, half, lo : lo + P] for b in range(2)],
               [db_q[:, b, jh, :] for b in range(2)], [db_s[:, b, jh, :] for b in range(2)], E4, E5)
            cols = slice(HALF * jh, HALF * jh + HALF)
            unsorted = acc[:].rearrange("p (u q r) -> p q u r", u=2, q=16)
            if on == "DVE":
                nc.vector.tensor_tensor(
                    out=res[:, cols].rearrange("p (q u r) -> p q u r", u=2, q=16),
                    in0=unsorted,
                    in1=m_sb[1, half][:, a, cols].rearrange("p (q u r) -> p q u r", u=2, q=16),
                    op=ALU.mult,
                )
            else:
                plain = plains.tile([P, HALF], F32, name="plain")
                nc.scalar.copy(out=plain[:].rearrange("p (q u r) -> p q u r", u=2, q=16), in_=unsorted)
                nc.gpsimd.tensor_tensor(out=res[:, cols], in0=plain[:], in1=m_sb[1, half][:, a, cols], op=ALU.mult)

        def s3(it):
            nc.sync.dma_start(out=out_1_v[it // 4][:, it % 4, :], in_=prod["res3", it][:])

        def p2(half, n, i, on="ACT"):
            if ("res2", half, n) not in prod:
                prod["res2", half, n] = raw4.tile([P, 2, HALF], F32, name="r4")
            acc = ps_m.tile([P, HALF], F32, name="acc")
            mx(acc, [z2_q[:, n, i, g, :] for g in range(2)], [z2_s[:, n, i, g, :] for g in range(2)],
               [w1_q[:, half, g, :] for g in range(2)], [w1_s[:, half, g, :] for g in range(2)], E5, E4)
            leave(prod["res2", half, n][:, i, :], acc[:], on)

        def s2(half, n):
            b, s0 = n // 2, 2 * (n % 2)
            nc.sync.dma_start(out=out_0_v[b][:, s0 : s0 + 2, HALF * half : HALF * half + HALF], in_=prod["res2", half, n][:])

        def ld(kind, i):
            if kind == "w":
                if i == 0:
                    for a in range(2):
                        k_sb[2, 0, a] = load(raw4, "r4", [1, U], BF16, k2_v[0][:, a : a + 1, :])
                        m_sb[2, 0, a] = load(raw4, "r4", [1, U], BF16, m2_v[0][:, a : a + 1, :])
                else:
                    k_sb[2, i] = load(raw4, "r4", [2, U], BF16, k2_v[i])
                    m_sb[2, i] = load(raw4, "r4", [2, U], BF16, m2_v[i])
            elif kind == "z":
                b, s0 = i // 2, 2 * (i % 2)
                z_sb[i] = load(raw8, "r8", [2, U], F32, z_v[b][:, s0 : s0 + 2, :])
                g_sb[i] = load(raw4, "r4", [2, U], BF16, g_v[b][:, s0 : s0 + 2, :])
            elif kind == "h":
                h_sb[i] = load(raw_h, "hm", [4, U], BF16, h_v[i])
            elif kind == "m":
                m_sb[1, i] = load(raw_h, "hm", [4, U], BF16, m1_v[i])
            else:
                k_sb[1, i] = load(raw8, "r8", [4, U], BF16, k1_v[i])

        ld("w", 2)
        ld("z", 0)
        ld("w", 0)
        ld("w", 3)
        ld("w", 1)
        ld("z", 1)
        ld("z", 3)
        ld("z", 2)
        ld("h", 0)
        ld("m", 1)
        ld("k", 1)
        ld("k", 0)
        ld("m", 0)
        ld("h", 1)
        with tc.manual_schedule():
            nc.scalar.copy(out=gain_row[0:1, 0:1], in_=gain_in[0:1, :])
            spread = ps_m.tile([P, HALF], F32, name="acc")
            nc.tensor.matmul(spread[:, 0:64], lhsT=ones[:], rhs=gain_row[:], start=True, stop=True)
            nc.scalar.copy(out=gain[:], in_=spread[:, 0:1])
            wm(2, 2)
            zs(0)
            wt(2, 2, ("ACT", "ACT"))
            zm(0)
            zt(0)
            wm(2, 0)
            zq(0)
            wm(2, 3)
            wt(2, 0, ("DVE", "ACT"))
            wt(2, 3)
            wm(2, 1)
            wt(2, 1)
            wq(2, 1)
            zs(1)
            p1(0, 1, 1)
            zm(1)
            p1(0, 0, 1)
            wq(2, 0)
            zt(1)
            p1(0, 0, 0)
            zs(3)
            zq(1)
            p1(0, 1, 0)
            tt(0)
            zm(3)
            p1(1, 1, 1)
            zs(2)
            zm(2)
            zt(3)
            p1(1, 1, 0, "DVE")
            p1(1, 0, 1)
            p1(1, 0, 0)
            zq(3)
            zt(2)
            hl(0, 1)
            bl(0, 0, "ACT")
            hl(0, 0)
            p1(3, 0, 0)
            p1(3, 1, 1)
            zq(2)
            hq(0)
            p1(3, 1, 0)
            wm(1, 1)
            tt(1)
            p1(2, 1, 1, "DVE")
            p1(2, 0, 1, "DVE")
            p1(3, 0, 1)
            p1(2, 1, 0, "DVE")
            tq(0)
            p1(2, 0, 0)
            wm(1, 0)
            wt(1, 2)
            wt(1, 3)
            tt(2)
            wq(1, 1)
            tt(3, ("ACT", "DVE"))
            hl(1, 0, "ACT")
            wt(1, 1)
            p2(1, 0, 0)
            hl(1, 1)
            p2(1, 0, 1)
            tq(1)
            bl(1, 0)
            wt(1, 0)
            bq(0, 0)
            p2(1, 1, 0, "DVE")
            wq(1, 0)
            bq(1, 0)
            s2(1, 0)
            p2(1, 1, 1)
            p2(1, 3, 0)
            p2(1, 3, 1)
            hq(1)
            bl(0, 1)
            bl(1, 1)
            p2(1, 2, 1)
            s2(1, 1)
            p2(1, 2, 0)
            bq(0, 1)
            p2(0, 3, 0)
            p2(0, 3, 1)
            s2(1, 3)
            p2(0, 0, 0)
            p2(0, 0, 1)
            s2(1, 2)
            p2(0, 1, 0)
            p2(0, 1, 1)
            bq(1, 1)
            s2(0, 3)
            s2(0, 0)
            p2(0, 2, 1)
            p2(0, 2, 0)
            p3(4, 0)
            p3(6, 0, "ACT")
            p3(4, 1)
            p3(6, 1)
            s2(0, 1)
            s2(0, 2)
            p3(3, 1)
            p3(2, 1, "ACT")
            p3(3, 0)
            p3(2, 0)
            p3(7, 0)
            p3(0, 1, "ACT")
            s3(4)
            s3(6)
            p3(7, 1)
            p3(0, 0)
            p3(1, 1)
            p3(1, 0)
            s3(3)
            p3(5, 0)
            p3(5, 1)
            s3(2)
            s3(7)
            s3(0)
            s3(1)
            s3(5)
